import numpy as np
import ml_dtypes


def mxq(x, axis, fmt="e4m3"):
    dtype, down = {"e4m3": (ml_dtypes.float8_e4m3fn, 7), "e5m2": (ml_dtypes.float8_e5m2, 14)}[fmt]
    v = np.moveaxis(np.asarray(x, np.float32).astype(ml_dtypes.bfloat16).astype(np.float64), axis, -1)
    blocks = v.reshape(v.shape[:-1] + (-1, 32))
    amax = np.abs(blocks).max(-1, keepdims=True)
    byte = np.maximum(np.where(amax > 0, np.frexp(amax)[1] - 1 + 127, 0) - down, 1)
    scale = np.exp2(byte - 127.0)
    codes = (blocks / scale).astype(np.float32).astype(dtype).astype(np.float64)
    return np.moveaxis((codes * scale).reshape(v.shape), -1, axis)


WIDE = False


def mx_kscale(k):
    if not WIDE:
        return np.ones(k)
    levels = np.array([10, -10, 5, -5, 0])
    a = np.random.permutation(np.resize(levels, k // 512 * 4)).reshape(k // 512, 4)
    idx = np.arange(k)
    return np.exp2(a[idx // 512, idx % 128 // 32])


BF16 = ml_dtypes.bfloat16


def bf(x):
    return np.asarray(x, np.float32).astype(BF16)


def f64(x):
    return np.asarray(x).astype(np.float64)


B, C, SQ, SK, H, HKV, D = 2, 2048, 256, 512, 8, 1, 256
HALF = D // 2


def apply_rope(x, sin, cos):
    x1, x2 = np.split(x, 2, axis=-2)
    return np.concatenate((x1 * cos - x2 * sin, x2 * cos + x1 * sin), axis=-2)


def setup_inputs():
    s = mx_kscale(C)
    return {"Xkv": bf(np.random.standard_normal((B, C, SK)) * s[:, None]),
            "sin_k": bf(np.random.uniform(-1.0, 1.0, (B, 1, HALF, SK))),
            "cos_k": bf(np.random.uniform(-1.0, 1.0, (B, 1, HALF, SK))),
            "Wk": bf(np.random.standard_normal((HKV * D, C)) * 1.7 / np.sqrt(C) / s),
            "Wv": bf(np.random.standard_normal((HKV * D, C)) * 2.0 / np.sqrt(C) / s)}


def reference(Xkv, sin_k, cos_k, Wk, Wv):
    xq = mxq(f64(Xkv), 1, "e4m3")
    k = (mxq(f64(Wk), 1, "e4m3") @ xq).reshape(B, HKV, D, SK)
    k = apply_rope(k, f64(sin_k), f64(cos_k))
    v = (mxq(f64(Wv), 1, "e4m3") @ xq).reshape(B, HKV, D, SK)
    return k, v

@@ -1,0 +1,152 @@
+from contextlib import ExitStack
+
+import concourse.mybir as mybir
+from concourse.masks import make_identity
+
+F32 = mybir.dt.float32
+BF16 = mybir.dt.bfloat16
+U32 = mybir.dt.uint32
+U8 = mybir.dt.uint8
+FP8X4 = mybir.dt.float8_e4m3fn_x4
+
+P = 128
+PACK = 4
+K_PASS = P * PACK
+PAIR = 2
+
+B = 2
+C = 2048
+S = 512
+D = 256
+PASSES = C // K_PASS
+ROW_TILES = 2 * D // P
+BANK_PASSES = 2
+
+SCALAR_POSITIONS = 256
+RUN = 4
+
+FLOPS = 2 * B * (2 * D) * C * S
+
+
+def tile_aneattention_pb_kernel(tc, Xkv, sin_k, cos_k, Wk, Wv, out_0, out_1):
+    nc = tc.nc
+    with ExitStack() as ctx:
+        keep = ctx.enter_context(tc.tile_pool(name="keep", bufs=1))
+        stage = ctx.enter_context(tc.tile_pool(name="stage", bufs=3))
+        results = ctx.enter_context(tc.tile_pool(name="results", bufs=2))
+        psum = ctx.enter_context(tc.psum_pool(name="psum", bufs=8))
+
+        identity = keep.tile([P, P], F32, name="identity")
+        make_identity(nc, identity[:])
+
+        w_rows = [Wk[0:P, :], Wk[P : 2 * P, :], Wv[0:P, :], Wv[P : 2 * P, :]]
+        w_raw = []
+        for t in range(ROW_TILES):
+            raw = keep.tile([P, C], BF16, name="w_raw%d" % t)
+            nc.sync.dma_start(out=raw[:], in_=w_rows[t])
+            w_raw.append(raw)
+
+        x_raw = {}
+        sin_sb = []
+        cos_sb = []
+        for b in range(B):
+            for g in range(PASSES):
+                raw = keep.tile([P, PACK, S], BF16, name="x_raw%d_%d" % (b, g))
+                rows = Xkv[b, g * K_PASS : (g + 1) * K_PASS, :]
+                nc.sync.dma_start(out=raw[:], in_=rows.rearrange("(p j) s -> p j s", j=PACK))
+                x_raw[(b, g)] = raw
+            sin_b = keep.tile([P, S], BF16, name="sin%d" % b)
+            nc.sync.dma_start(out=sin_b[:], in_=sin_k[b, 0, :, :])
+            sin_sb.append(sin_b)
+            cos_b = keep.tile([P, S], BF16, name="cos%d" % b)
+            nc.sync.dma_start(out=cos_b[:], in_=cos_k[b, 0, :, :])
+            cos_sb.append(cos_b)
+
+        w_codes = keep.tile([P, ROW_TILES, PASSES, P], U32, name="w_codes", align_bytes=64)
+        w_scales = keep.tile([P, ROW_TILES, PASSES, P], U8, name="w_scales", align_bytes=64)
+        for t in range(ROW_TILES):
+            words = w_raw[t][:].bitcast(F32).rearrange("m (g p u) -> m g u p", g=PASSES, u=PAIR)
+            w_grouped = stage.tile([P, PASSES, P, PACK], BF16, name="w_grouped", align_bytes=64)
+            grouped_words = w_grouped[:].rearrange("p g m j -> p (g m j)").bitcast(F32)
+            grouped_words = grouped_words.rearrange("p (g m u) -> p g m u", g=PASSES, u=PAIR)
+            for first in range(0, PASSES, BANK_PASSES):
+                bank = psum.tile([P, BANK_PASSES, PAIR, P], F32, name="w_bank", tag="bank")
+                for i in range(BANK_PASSES):
+                    for u in range(PAIR):
+                        nc.tensor.transpose(bank[:, i, u, :], words[:, first + i, u, :], identity[:])
+                nc.scalar.copy(
+                    out=grouped_words[:, first : first + BANK_PASSES, :, :],
+                    in_=bank[:].rearrange("p g u m -> p g m u"),
+                )
+            nc.vector.quantize_mx(
+                out=w_codes[:, t, :, :].rearrange("p g m -> p (g m)").bitcast(FP8X4),
+                scales=w_scales[:, t, :, :].rearrange("p g m -> p (g m)"),
+                in_=w_grouped[:].rearrange("p g m j -> p (g m j)"),
+            )
+
+        x_codes = keep.tile([P, B, PASSES, S], U32, name="x_codes", align_bytes=64)
+        x_scales = keep.tile([P, B, PASSES, S], U8, name="x_scales", align_bytes=64)
+        x_grouped = {}
+        sums = {}
+
+        def regroup(b, g):
+            grouped = stage.tile([P, S, PACK], BF16, name="x_grouped", align_bytes=64)
+            dst = grouped[:].rearrange("p (c i) j -> p c j i", i=RUN)
+            src = x_raw[(b, g)][:].rearrange("p j (c i) -> p c j i", i=RUN)
+            cut = SCALAR_POSITIONS // RUN
+            nc.scalar.copy(out=dst[:, :cut, :, :], in_=src[:, :cut, :, :])
+            nc.vector.tensor_copy(out=dst[:, cut:, :, :], in_=src[:, cut:, :, :])
+            x_grouped[(b, g)] = grouped
+
+        def quantise(b, g):
+            nc.vector.quantize_mx(
+                out=x_codes[:, b, g, :].bitcast(FP8X4),
+                scales=x_scales[:, b, g, :],
+                in_=x_grouped[(b, g)][:].rearrange("p s j -> p (s j)"),
+            )
+
+        def multiply(b, g):
+            for t in range(ROW_TILES):
+                if g == 0:
+                    sums[(b, t)] = psum.tile([P, S], F32, name="sums", tag="bank")
+                nc.tensor.matmul_mx(
+                    out=sums[(b, t)][:],
+                    lhsT=w_codes[:, t, g, :].bitcast(FP8X4),
+                    lhsT_scale=w_scales[:, t, g, :],
+                    rhs=x_codes[:, b, g, :].bitcast(FP8X4),
+                    rhs_scale=x_scales[:, b, g, :],
+                    start=(g == 0),
+                    stop=(g == PASSES - 1),
+                )
+
+        def finish(b):
+            for half in range(2):
+                v_sb = results.tile([P, S], F32, name="v_sb")
+                nc.scalar.copy(out=v_sb[:], in_=sums[(b, 2 + half)][:])
+                nc.sync.dma_start(out=out_1[b, 0, half * P : (half + 1) * P, :], in_=v_sb[:])
+            x1 = sums[(b, 0)]
+            x2 = sums[(b, 1)]
+            x1_cos = results.tile([P, S], F32, name="x1_cos")
+            x2_sin = results.tile([P, S], F32, name="x2_sin")
+            x2_cos = results.tile([P, S], F32, name="x2_cos")
+            x1_sin = results.tile([P, S], F32, name="x1_sin")
+            nc.vector.tensor_mul(out=x1_cos[:], in0=x1[:], in1=cos_sb[b][:])
+            nc.vector.tensor_mul(out=x2_sin[:], in0=x2[:], in1=sin_sb[b][:])
+            nc.vector.tensor_mul(out=x2_cos[:], in0=x2[:], in1=cos_sb[b][:])
+            nc.vector.tensor_mul(out=x1_sin[:], in0=x1[:], in1=sin_sb[b][:])
+            top = results.tile([P, S], F32, name="top")
+            nc.vector.tensor_sub(out=top[:], in0=x1_cos[:], in1=x2_sin[:])
+            nc.sync.dma_start(out=out_0[b, 0, 0:P, :], in_=top[:])
+            bottom = results.tile([P, S], F32, name="bottom")
+            nc.vector.tensor_add(out=bottom[:], in0=x2_cos[:], in1=x1_sin[:])
+            nc.sync.dma_start(out=out_0[b, 0, P : 2 * P, :], in_=bottom[:])
+
+        chunks = [(b, g) for b in range(B) for g in range(PASSES)]
+        for step in range(len(chunks) + 2):
+            if step < len(chunks):
+                regroup(*chunks[step])
+            if 1 <= step <= len(chunks):
+                quantise(*chunks[step - 1])
+                multiply(*chunks[step - 1])
+            if step >= 2 and chunks[step - 2][1] == PASSES - 1:
+                finish(chunks[step - 2][0])

@@ -22,7 +22,7 @@ PASSES = C // K_PASS
 ROW_TILES = 2 * D // P
 BANK_PASSES = 2
 
-SCALAR_POSITIONS = 256
+SCALAR_POSITIONS = (256, 320)
 RUN = 4
 
 FLOPS = 2 * B * (2 * D) * C * S
@@ -34,7 +34,9 @@ def tile_aneattention_pb_kernel(tc, Xkv, sin_k, cos_k, Wk, Wv, out_0, out_1):
         keep = ctx.enter_context(tc.tile_pool(name="keep", bufs=1))
         stage = ctx.enter_context(tc.tile_pool(name="stage", bufs=3))
         results = ctx.enter_context(tc.tile_pool(name="results", bufs=2))
+        values = ctx.enter_context(tc.tile_pool(name="values", bufs=4))
         psum = ctx.enter_context(tc.psum_pool(name="psum", bufs=8))
+        ctx.enter_context(tc.manual_schedule())
 
         identity = keep.tile([P, P], F32, name="identity")
         make_identity(nc, identity[:])
@@ -93,7 +95,7 @@ def tile_aneattention_pb_kernel(tc, Xkv, sin_k, cos_k, Wk, Wv, out_0, out_1):
             grouped = stage.tile([P, S, PACK], BF16, name="x_grouped", align_bytes=64)
             dst = grouped[:].rearrange("p (c i) j -> p c j i", i=RUN)
             src = x_raw[(b, g)][:].rearrange("p j (c i) -> p c j i", i=RUN)
-            cut = SCALAR_POSITIONS // RUN
+            cut = SCALAR_POSITIONS[b] // RUN
             nc.scalar.copy(out=dst[:, :cut, :, :], in_=src[:, :cut, :, :])
             nc.vector.tensor_copy(out=dst[:, cut:, :, :], in_=src[:, cut:, :, :])
             x_grouped[(b, g)] = grouped
@@ -119,34 +121,52 @@ def tile_aneattention_pb_kernel(tc, Xkv, sin_k, cos_k, Wk, Wv, out_0, out_1):
                     stop=(g == PASSES - 1),
                 )
 
-        def finish(b):
+        def store_values(b):
             for half in range(2):
-                v_sb = results.tile([P, S], F32, name="v_sb")
+                v_sb = values.tile([P, S], F32, name="v_sb")
                 nc.scalar.copy(out=v_sb[:], in_=sums[(b, 2 + half)][:])
                 nc.sync.dma_start(out=out_1[b, 0, half * P : (half + 1) * P, :], in_=v_sb[:])
+
+        def rotation_parts(b):
             x1 = sums[(b, 0)]
             x2 = sums[(b, 1)]
             x1_cos = results.tile([P, S], F32, name="x1_cos")
             x2_sin = results.tile([P, S], F32, name="x2_sin")
             x2_cos = results.tile([P, S], F32, name="x2_cos")
             x1_sin = results.tile([P, S], F32, name="x1_sin")
-            nc.vector.tensor_mul(out=x1_cos[:], in0=x1[:], in1=cos_sb[b][:])
-            nc.vector.tensor_mul(out=x2_sin[:], in0=x2[:], in1=sin_sb[b][:])
-            nc.vector.tensor_mul(out=x2_cos[:], in0=x2[:], in1=cos_sb[b][:])
-            nc.vector.tensor_mul(out=x1_sin[:], in0=x1[:], in1=sin_sb[b][:])
-            top = results.tile([P, S], F32, name="top")
-            nc.vector.tensor_sub(out=top[:], in0=x1_cos[:], in1=x2_sin[:])
-            nc.sync.dma_start(out=out_0[b, 0, 0:P, :], in_=top[:])
-            bottom = results.tile([P, S], F32, name="bottom")
-            nc.vector.tensor_add(out=bottom[:], in0=x2_cos[:], in1=x1_sin[:])
-            nc.sync.dma_start(out=out_0[b, 0, P : 2 * P, :], in_=bottom[:])
+
+            def products_of_top():
+                nc.vector.tensor_mul(out=x1_cos[:], in0=x1[:], in1=cos_sb[b][:])
+                nc.vector.tensor_mul(out=x2_sin[:], in0=x2[:], in1=sin_sb[b][:])
+
+            def products_of_bottom():
+                nc.vector.tensor_mul(out=x2_cos[:], in0=x2[:], in1=cos_sb[b][:])
+                nc.vector.tensor_mul(out=x1_sin[:], in0=x1[:], in1=sin_sb[b][:])
+
+            def sums_and_stores():
+                top = results.tile([P, S], F32, name="top")
+                nc.vector.tensor_sub(out=top[:], in0=x1_cos[:], in1=x2_sin[:])
+                nc.sync.dma_start(out=out_0[b, 0, 0:P, :], in_=top[:])
+                bottom = results.tile([P, S], F32, name="bottom")
+                nc.vector.tensor_add(out=bottom[:], in0=x2_cos[:], in1=x1_sin[:])
+                nc.sync.dma_start(out=out_0[b, 0, P : 2 * P, :], in_=bottom[:])
+
+            return [products_of_top, products_of_bottom, sums_and_stores]
 
         chunks = [(b, g) for b in range(B) for g in range(PASSES)]
-        for step in range(len(chunks) + 2):
+        first_part_step = PASSES + 2
+        parts = []
+        for step in range(len(chunks) + 1):
             if step < len(chunks):
                 regroup(*chunks[step])
-            if 1 <= step <= len(chunks):
+            if step >= 1:
                 quantise(*chunks[step - 1])
                 multiply(*chunks[step - 1])
-            if step >= 2 and chunks[step - 2][1] == PASSES - 1:
-                finish(chunks[step - 2][0])
+            if step == first_part_step:
+                parts = rotation_parts(0)
+            if step >= first_part_step:
+                parts[step - first_part_step]()
+        store_values(0)
+        store_values(1)
+        for part in rotation_parts(1):
+            part()

@@ -33,7 +33,7 @@ def tile_aneattention_pb_kernel(tc, Xkv, sin_k, cos_k, Wk, Wv, out_0, out_1):
     with ExitStack() as ctx:
         keep = ctx.enter_context(tc.tile_pool(name="keep", bufs=1))
         stage = ctx.enter_context(tc.tile_pool(name="stage", bufs=3))
-        results = ctx.enter_context(tc.tile_pool(name="results", bufs=2))
+        results = ctx.enter_context(tc.tile_pool(name="results", bufs=4))
         values = ctx.enter_context(tc.tile_pool(name="values", bufs=4))
         psum = ctx.enter_context(tc.psum_pool(name="psum", bufs=8))
         ctx.enter_context(tc.manual_schedule())
@@ -127,46 +127,38 @@ def tile_aneattention_pb_kernel(tc, Xkv, sin_k, cos_k, Wk, Wv, out_0, out_1):
                 nc.scalar.copy(out=v_sb[:], in_=sums[(b, 2 + half)][:])
                 nc.sync.dma_start(out=out_1[b, 0, half * P : (half + 1) * P, :], in_=v_sb[:])
 
-        def rotation_parts(b):
-            x1 = sums[(b, 0)]
-            x2 = sums[(b, 1)]
-            x1_cos = results.tile([P, S], F32, name="x1_cos")
-            x2_sin = results.tile([P, S], F32, name="x2_sin")
-            x2_cos = results.tile([P, S], F32, name="x2_cos")
-            x1_sin = results.tile([P, S], F32, name="x1_sin")
+        products = {}
 
-            def products_of_top():
-                nc.vector.tensor_mul(out=x1_cos[:], in0=x1[:], in1=cos_sb[b][:])
-                nc.vector.tensor_mul(out=x2_sin[:], in0=x2[:], in1=sin_sb[b][:])
+        def multiply_by_tables(b, half):
+            with_cos = results.tile([P, S], F32, name="with_cos")
+            with_sin = results.tile([P, S], F32, name="with_sin")
+            nc.vector.tensor_mul(out=with_cos[:], in0=sums[(b, half)][:], in1=cos_sb[b][:])
+            nc.vector.tensor_mul(out=with_sin[:], in0=sums[(b, 1 - half)][:], in1=sin_sb[b][:])
+            products[(b, half)] = (with_cos, with_sin)
 
-            def products_of_bottom():
-                nc.vector.tensor_mul(out=x2_cos[:], in0=x2[:], in1=cos_sb[b][:])
-                nc.vector.tensor_mul(out=x1_sin[:], in0=x1[:], in1=sin_sb[b][:])
-
-            def sums_and_stores():
-                top = results.tile([P, S], F32, name="top")
-                nc.vector.tensor_sub(out=top[:], in0=x1_cos[:], in1=x2_sin[:])
-                nc.sync.dma_start(out=out_0[b, 0, 0:P, :], in_=top[:])
-                bottom = results.tile([P, S], F32, name="bottom")
-                nc.vector.tensor_add(out=bottom[:], in0=x2_cos[:], in1=x1_sin[:])
-                nc.sync.dma_start(out=out_0[b, 0, P : 2 * P, :], in_=bottom[:])
-
-            return [products_of_top, products_of_bottom, sums_and_stores]
+        def combine(engine, b, half):
+            with_cos, with_sin = products[(b, half)]
+            rotated = results.tile([P, S], F32, name="rotated")
+            op = mybir.AluOpType.subtract if half == 0 else mybir.AluOpType.add
+            engine.tensor_tensor(out=rotated[:], in0=with_cos[:], in1=with_sin[:], op=op)
+            nc.sync.dma_start(out=out_0[b, 0, half * P : (half + 1) * P, :], in_=rotated[:])
 
         chunks = [(b, g) for b in range(B) for g in range(PASSES)]
-        first_part_step = PASSES + 2
-        parts = []
         for step in range(len(chunks) + 1):
             if step < len(chunks):
                 regroup(*chunks[step])
             if step >= 1:
                 quantise(*chunks[step - 1])
                 multiply(*chunks[step - 1])
-            if step == first_part_step:
-                parts = rotation_parts(0)
-            if step >= first_part_step:
-                parts[step - first_part_step]()
+            if step == PASSES + 2:
+                multiply_by_tables(0, 0)
+
         store_values(0)
+        multiply_by_tables(0, 1)
+        combine(nc.gpsimd, 0, 0)
+        multiply_by_tables(1, 0)
         store_values(1)
-        for part in rotation_parts(1):
-            part()
+        combine(nc.gpsimd, 0, 1)
+        multiply_by_tables(1, 1)
+        combine(nc.gpsimd, 1, 0)
+        combine(nc.vector, 1, 1)

@@ -22,7 +22,7 @@ PASSES = C // K_PASS
 ROW_TILES = 2 * D // P
 BANK_PASSES = 2
 
-SCALAR_POSITIONS = (256, 320)
+SCALAR_POSITIONS = (160, 320)
 RUN = 4
 
 FLOPS = 2 * B * (2 * D) * C * S
@@ -35,44 +35,59 @@ def tile_aneattention_pb_kernel(tc, Xkv, sin_k, cos_k, Wk, Wv, out_0, out_1):
         stage = ctx.enter_context(tc.tile_pool(name="stage", bufs=3))
         results = ctx.enter_context(tc.tile_pool(name="results", bufs=4))
         values = ctx.enter_context(tc.tile_pool(name="values", bufs=4))
-        psum = ctx.enter_context(tc.psum_pool(name="psum", bufs=8))
+        psum = ctx.enter_context(tc.psum_pool(name="psum", bufs=1))
         ctx.enter_context(tc.manual_schedule())
 
         identity = keep.tile([P, P], F32, name="identity")
         make_identity(nc, identity[:])
 
-        w_rows = [Wk[0:P, :], Wk[P : 2 * P, :], Wv[0:P, :], Wv[P : 2 * P, :]]
-        w_raw = []
-        for t in range(ROW_TILES):
-            raw = keep.tile([P, C], BF16, name="w_raw%d" % t)
-            nc.sync.dma_start(out=raw[:], in_=w_rows[t])
-            w_raw.append(raw)
+        units = []
+        for i in range(PASSES):
+            units.append(("w", i))
+            units.append(("x", 0, i))
+        for g in range(PASSES):
+            units.append(("x", 1, g))
 
+        w_rows = [Wk[0:P, :], Wk[P : 2 * P, :], Wv[0:P, :], Wv[P : 2 * P, :]]
+        w_raw = {}
         x_raw = {}
-        sin_sb = []
-        cos_sb = []
-        for b in range(B):
-            for g in range(PASSES):
+        sin_sb = {}
+        cos_sb = {}
+        for unit in units:
+            if unit[0] == "w":
+                t = unit[1]
+                raw = keep.tile([P, C], BF16, name="w_raw%d" % t)
+                nc.sync.dma_start(out=raw[:], in_=w_rows[t])
+                w_raw[t] = raw
+            else:
+                b, g = unit[1], unit[2]
                 raw = keep.tile([P, PACK, S], BF16, name="x_raw%d_%d" % (b, g))
                 rows = Xkv[b, g * K_PASS : (g + 1) * K_PASS, :]
                 nc.sync.dma_start(out=raw[:], in_=rows.rearrange("(p j) s -> p j s", j=PACK))
                 x_raw[(b, g)] = raw
-            sin_b = keep.tile([P, S], BF16, name="sin%d" % b)
-            nc.sync.dma_start(out=sin_b[:], in_=sin_k[b, 0, :, :])
-            sin_sb.append(sin_b)
-            cos_b = keep.tile([P, S], BF16, name="cos%d" % b)
-            nc.sync.dma_start(out=cos_b[:], in_=cos_k[b, 0, :, :])
-            cos_sb.append(cos_b)
+                if g == PASSES - 1:
+                    sin_b = keep.tile([P, S], BF16, name="sin%d" % b)
+                    nc.sync.dma_start(out=sin_b[:], in_=sin_k[b, 0, :, :])
+                    sin_sb[b] = sin_b
+                    cos_b = keep.tile([P, S], BF16, name="cos%d" % b)
+                    nc.sync.dma_start(out=cos_b[:], in_=cos_k[b, 0, :, :])
+                    cos_sb[b] = cos_b
 
         w_codes = keep.tile([P, ROW_TILES, PASSES, P], U32, name="w_codes", align_bytes=64)
         w_scales = keep.tile([P, ROW_TILES, PASSES, P], U8, name="w_scales", align_bytes=64)
-        for t in range(ROW_TILES):
+        x_codes = keep.tile([P, B, PASSES, S], U32, name="x_codes", align_bytes=64)
+        x_scales = keep.tile([P, B, PASSES, S], U8, name="x_scales", align_bytes=64)
+        grouped_of = {}
+        sums = {}
+
+        def regroup_weights(t):
             words = w_raw[t][:].bitcast(F32).rearrange("m (g p u) -> m g u p", g=PASSES, u=PAIR)
             w_grouped = stage.tile([P, PASSES, P, PACK], BF16, name="w_grouped", align_bytes=64)
             grouped_words = w_grouped[:].rearrange("p g m j -> p (g m j)").bitcast(F32)
             grouped_words = grouped_words.rearrange("p (g m u) -> p g m u", g=PASSES, u=PAIR)
             for first in range(0, PASSES, BANK_PASSES):
-                bank = psum.tile([P, BANK_PASSES, PAIR, P], F32, name="w_bank", tag="bank")
+                number = 4 + 2 * (t % 2) + first // BANK_PASSES
+                bank = psum.tile([P, BANK_PASSES, PAIR, P], F32, name="w_bank", tag="bank%d" % number)
                 for i in range(BANK_PASSES):
                     for u in range(PAIR):
                         nc.tensor.transpose(bank[:, i, u, :], words[:, first + i, u, :], identity[:])
@@ -80,52 +95,66 @@ def tile_aneattention_pb_kernel(tc, Xkv, sin_k, cos_k, Wk, Wv, out_0, out_1):
                     out=grouped_words[:, first : first + BANK_PASSES, :, :],
                     in_=bank[:].rearrange("p g u m -> p g m u"),
                 )
-            nc.vector.quantize_mx(
-                out=w_codes[:, t, :, :].rearrange("p g m -> p (g m)").bitcast(FP8X4),
-                scales=w_scales[:, t, :, :].rearrange("p g m -> p (g m)"),
-                in_=w_grouped[:].rearrange("p g m j -> p (g m j)"),
-            )
+            grouped_of[("w", t)] = w_grouped
 
-        x_codes = keep.tile([P, B, PASSES, S], U32, name="x_codes", align_bytes=64)
-        x_scales = keep.tile([P, B, PASSES, S], U8, name="x_scales", align_bytes=64)
-        x_grouped = {}
-        sums = {}
-
-        def regroup(b, g):
+        def regroup_chunk(b, g):
             grouped = stage.tile([P, S, PACK], BF16, name="x_grouped", align_bytes=64)
             dst = grouped[:].rearrange("p (c i) j -> p c j i", i=RUN)
             src = x_raw[(b, g)][:].rearrange("p j (c i) -> p c j i", i=RUN)
             cut = SCALAR_POSITIONS[b] // RUN
             nc.scalar.copy(out=dst[:, :cut, :, :], in_=src[:, :cut, :, :])
             nc.vector.tensor_copy(out=dst[:, cut:, :, :], in_=src[:, cut:, :, :])
-            x_grouped[(b, g)] = grouped
+            grouped_of[("x", b, g)] = grouped
 
-        def quantise(b, g):
-            nc.vector.quantize_mx(
-                out=x_codes[:, b, g, :].bitcast(FP8X4),
-                scales=x_scales[:, b, g, :],
-                in_=x_grouped[(b, g)][:].rearrange("p s j -> p (s j)"),
-            )
+        def regroup(unit):
+            if unit[0] == "w":
+                regroup_weights(unit[1])
+            else:
+                regroup_chunk(unit[1], unit[2])
 
-        def multiply(b, g):
-            for t in range(ROW_TILES):
-                if g == 0:
-                    sums[(b, t)] = psum.tile([P, S], F32, name="sums", tag="bank")
-                nc.tensor.matmul_mx(
-                    out=sums[(b, t)][:],
-                    lhsT=w_codes[:, t, g, :].bitcast(FP8X4),
-                    lhsT_scale=w_scales[:, t, g, :],
-                    rhs=x_codes[:, b, g, :].bitcast(FP8X4),
-                    rhs_scale=x_scales[:, b, g, :],
-                    start=(g == 0),
-                    stop=(g == PASSES - 1),
+        def quantise(unit):
+            if unit[0] == "w":
+                t = unit[1]
+                nc.vector.quantize_mx(
+                    out=w_codes[:, t, :, :].rearrange("p g m -> p (g m)").bitcast(FP8X4),
+                    scales=w_scales[:, t, :, :].rearrange("p g m -> p (g m)"),
+                    in_=grouped_of[unit][:].rearrange("p g m j -> p (g m j)"),
+                )
+            else:
+                b, g = unit[1], unit[2]
+                nc.vector.quantize_mx(
+                    out=x_codes[:, b, g, :].bitcast(FP8X4),
+                    scales=x_scales[:, b, g, :],
+                    in_=grouped_of[unit][:].rearrange("p s j -> p (s j)"),
                 )
 
-        def store_values(b):
-            for half in range(2):
-                v_sb = values.tile([P, S], F32, name="v_sb")
-                nc.scalar.copy(out=v_sb[:], in_=sums[(b, 2 + half)][:])
-                nc.sync.dma_start(out=out_1[b, 0, half * P : (half + 1) * P, :], in_=v_sb[:])
+        quantised = set()
+        multiplied = set()
+
+        def multiply_what_is_ready(unit):
+            quantised.add(unit)
+            for b in range(B):
+                for g in range(PASSES):
+                    for t in range(ROW_TILES):
+                        if (b, g, t) in multiplied or ("x", b, g) not in quantised or ("w", t) not in quantised:
+                            continue
+                        multiplied.add((b, g, t))
+                        if g == 0:
+                            sums[(b, t)] = psum.tile([P, S], F32, name="sums", tag="bank%d" % (4 * b + t))
+                        nc.tensor.matmul_mx(
+                            out=sums[(b, t)][:],
+                            lhsT=w_codes[:, t, g, :].bitcast(FP8X4),
+                            lhsT_scale=w_scales[:, t, g, :],
+                            rhs=x_codes[:, b, g, :].bitcast(FP8X4),
+                            rhs_scale=x_scales[:, b, g, :],
+                            start=(g == 0),
+                            stop=(g == PASSES - 1),
+                        )
+
+        def store_values(b, half):
+            v_sb = values.tile([P, S], F32, name="v_sb")
+            nc.scalar.copy(out=v_sb[:], in_=sums[(b, 2 + half)][:])
+            nc.sync.dma_start(out=out_1[b, 0, half * P : (half + 1) * P, :], in_=v_sb[:])
 
         products = {}
 
@@ -143,22 +172,23 @@ def tile_aneattention_pb_kernel(tc, Xkv, sin_k, cos_k, Wk, Wv, out_0, out_1):
             engine.tensor_tensor(out=rotated[:], in0=with_cos[:], in1=with_sin[:], op=op)
             nc.sync.dma_start(out=out_0[b, 0, half * P : (half + 1) * P, :], in_=rotated[:])
 
-        chunks = [(b, g) for b in range(B) for g in range(PASSES)]
-        for step in range(len(chunks) + 1):
-            if step < len(chunks):
-                regroup(*chunks[step])
-            if step >= 1:
-                quantise(*chunks[step - 1])
-                multiply(*chunks[step - 1])
-            if step == PASSES + 2:
-                multiply_by_tables(0, 0)
+        last = len(units) - 1
+        for step in range(len(units) + 2):
+            if step <= last:
+                regroup(units[step])
+            if 1 <= step <= last + 1:
+                quantise(units[step - 1])
+            if step >= 2:
+                multiply_what_is_ready(units[step - 2])
+            if step in (last - 1, last):
+                half = step - (last - 1)
+                multiply_by_tables(0, half)
+                combine(nc.gpsimd, 0, half)
+                store_values(0, half)
 
-        store_values(0)
-        multiply_by_tables(0, 1)
-        combine(nc.gpsimd, 0, 0)
         multiply_by_tables(1, 0)
-        store_values(1)
-        combine(nc.gpsimd, 0, 1)
-        multiply_by_tables(1, 1)
+        store_values(1, 0)
+        store_values(1, 1)
         combine(nc.gpsimd, 1, 0)
+        multiply_by_tables(1, 1)
         combine(nc.vector, 1, 1)

@@ -22,7 +22,9 @@ PASSES = C // K_PASS
 ROW_TILES = 2 * D // P
 BANK_PASSES = 2
 
-SCALAR_POSITIONS = (160, 320)
+SCALAR_POSITIONS = ((160, 160, 160, 128), (288, 320, 384, 352))
+TABLES_BEHIND = ((1, 1), (1, 3))
+PASS_LAG = 3
 RUN = 4
 
 FLOPS = 2 * B * (2 * D) * C * S
@@ -65,13 +67,14 @@ def tile_aneattention_pb_kernel(tc, Xkv, sin_k, cos_k, Wk, Wv, out_0, out_1):
                 rows = Xkv[b, g * K_PASS : (g + 1) * K_PASS, :]
                 nc.sync.dma_start(out=raw[:], in_=rows.rearrange("(p j) s -> p j s", j=PACK))
                 x_raw[(b, g)] = raw
-                if g == PASSES - 1:
-                    sin_b = keep.tile([P, S], BF16, name="sin%d" % b)
-                    nc.sync.dma_start(out=sin_b[:], in_=sin_k[b, 0, :, :])
-                    sin_sb[b] = sin_b
-                    cos_b = keep.tile([P, S], BF16, name="cos%d" % b)
-                    nc.sync.dma_start(out=cos_b[:], in_=cos_k[b, 0, :, :])
-                    cos_sb[b] = cos_b
+                if (b, g) in TABLES_BEHIND:
+                    tb = TABLES_BEHIND.index((b, g))
+                    sin_b = keep.tile([P, S], BF16, name="sin%d" % tb)
+                    nc.sync.dma_start(out=sin_b[:], in_=sin_k[tb, 0, :, :])
+                    sin_sb[tb] = sin_b
+                    cos_b = keep.tile([P, S], BF16, name="cos%d" % tb)
+                    nc.sync.dma_start(out=cos_b[:], in_=cos_k[tb, 0, :, :])
+                    cos_sb[tb] = cos_b
 
         w_codes = keep.tile([P, ROW_TILES, PASSES, P], U32, name="w_codes", align_bytes=64)
         w_scales = keep.tile([P, ROW_TILES, PASSES, P], U8, name="w_scales", align_bytes=64)
@@ -101,9 +104,10 @@ def tile_aneattention_pb_kernel(tc, Xkv, sin_k, cos_k, Wk, Wv, out_0, out_1):
             grouped = stage.tile([P, S, PACK], BF16, name="x_grouped", align_bytes=64)
             dst = grouped[:].rearrange("p (c i) j -> p c j i", i=RUN)
             src = x_raw[(b, g)][:].rearrange("p j (c i) -> p c j i", i=RUN)
-            cut = SCALAR_POSITIONS[b] // RUN
+            cut = SCALAR_POSITIONS[b][g] // RUN
             nc.scalar.copy(out=dst[:, :cut, :, :], in_=src[:, :cut, :, :])
-            nc.vector.tensor_copy(out=dst[:, cut:, :, :], in_=src[:, cut:, :, :])
+            if cut < S // RUN:
+                nc.vector.tensor_copy(out=dst[:, cut:, :, :], in_=src[:, cut:, :, :])
             grouped_of[("x", b, g)] = grouped
 
         def regroup(unit):
@@ -173,13 +177,13 @@ def tile_aneattention_pb_kernel(tc, Xkv, sin_k, cos_k, Wk, Wv, out_0, out_1):
             nc.sync.dma_start(out=out_0[b, 0, half * P : (half + 1) * P, :], in_=rotated[:])
 
         last = len(units) - 1
-        for step in range(len(units) + 2):
+        for step in range(len(units) + PASS_LAG):
             if step <= last:
                 regroup(units[step])
             if 1 <= step <= last + 1:
                 quantise(units[step - 1])
-            if step >= 2:
-                multiply_what_is_ready(units[step - 2])
+            if step >= PASS_LAG:
+                multiply_what_is_ready(units[step - PASS_LAG])
             if step in (last - 1, last):
                 half = step - (last - 1)
                 multiply_by_tables(0, half)

@@ -22,7 +22,7 @@ PASSES = C // K_PASS
 ROW_TILES = 2 * D // P
 BANK_PASSES = 2
 
-SCALAR_POSITIONS = ((160, 160, 160, 128), (288, 320, 384, 352))
+SCALAR_POSITIONS = ((160, 160, 160, 160), (288, 288, 416, 416))
 TABLES_BEHIND = ((1, 1), (1, 3))
 PASS_LAG = 3
 RUN = 4
@@ -106,8 +106,7 @@ def tile_aneattention_pb_kernel(tc, Xkv, sin_k, cos_k, Wk, Wv, out_0, out_1):
             src = x_raw[(b, g)][:].rearrange("p j (c i) -> p c j i", i=RUN)
             cut = SCALAR_POSITIONS[b][g] // RUN
             nc.scalar.copy(out=dst[:, :cut, :, :], in_=src[:, :cut, :, :])
-            if cut < S // RUN:
-                nc.vector.tensor_copy(out=dst[:, cut:, :, :], in_=src[:, cut:, :, :])
+            nc.vector.tensor_copy(out=dst[:, cut:, :, :], in_=src[:, cut:, :, :])
             grouped_of[("x", b, g)] = grouped
 
         def regroup(unit):
@@ -180,6 +179,9 @@ def tile_aneattention_pb_kernel(tc, Xkv, sin_k, cos_k, Wk, Wv, out_0, out_1):
         for step in range(len(units) + PASS_LAG):
             if step <= last:
                 regroup(units[step])
+            if step == last:
+                store_values(0, 0)
+                store_values(0, 1)
             if 1 <= step <= last + 1:
                 quantise(units[step - 1])
             if step >= PASS_LAG:
@@ -188,7 +190,6 @@ def tile_aneattention_pb_kernel(tc, Xkv, sin_k, cos_k, Wk, Wv, out_0, out_1):
                 half = step - (last - 1)
                 multiply_by_tables(0, half)
                 combine(nc.gpsimd, 0, half)
-                store_values(0, half)
 
         multiply_by_tables(1, 0)
         store_values(1, 0)

from contextlib import ExitStack

import concourse.mybir as mybir
from concourse.masks import make_identity

F32 = mybir.dt.float32
BF16 = mybir.dt.bfloat16
U32 = mybir.dt.uint32
U8 = mybir.dt.uint8
FP8X4 = mybir.dt.float8_e4m3fn_x4

P = 128
PACK = 4
K_PASS = P * PACK
PAIR = 2

B = 2
C = 2048
S = 512
D = 256
PASSES = C // K_PASS
ROW_TILES = 2 * D // P
BANK_PASSES = 2

SCALAR_POSITIONS = ((160, 160, 160, 160), (288, 288, 416, 416))
TABLES_BEHIND = ((1, 1), (1, 3))
PASS_LAG = 3
RUN = 4

FLOPS = 2 * B * (2 * D) * C * S


def tile_aneattention_pb_kernel(tc, Xkv, sin_k, cos_k, Wk, Wv, out_0, out_1):
    nc = tc.nc
    with ExitStack() as ctx:
        keep = ctx.enter_context(tc.tile_pool(name="keep", bufs=1))
        stage = ctx.enter_context(tc.tile_pool(name="stage", bufs=3))
        results = ctx.enter_context(tc.tile_pool(name="results", bufs=4))
        values = ctx.enter_context(tc.tile_pool(name="values", bufs=4))
        psum = ctx.enter_context(tc.psum_pool(name="psum", bufs=1))
        ctx.enter_context(tc.manual_schedule())

        identity = keep.tile([P, P], F32, name="identity")
        make_identity(nc, identity[:])

        units = []
        for i in range(PASSES):
            units.append(("w", i))
            units.append(("x", 0, i))
        for g in range(PASSES):
            units.append(("x", 1, g))

        w_rows = [Wk[0:P, :], Wk[P : 2 * P, :], Wv[0:P, :], Wv[P : 2 * P, :]]
        w_raw = {}
        x_raw = {}
        sin_sb = {}
        cos_sb = {}
        for unit in units:
            if unit[0] == "w":
                t = unit[1]
                raw = keep.tile([P, C], BF16, name="w_raw%d" % t)
                nc.sync.dma_start(out=raw[:], in_=w_rows[t])
                w_raw[t] = raw
            else:
                b, g = unit[1], unit[2]
                raw = keep.tile([P, PACK, S], BF16, name="x_raw%d_%d" % (b, g))
                rows = Xkv[b, g * K_PASS : (g + 1) * K_PASS, :]
                nc.sync.dma_start(out=raw[:], in_=rows.rearrange("(p j) s -> p j s", j=PACK))
                x_raw[(b, g)] = raw
                if (b, g) in TABLES_BEHIND:
                    tb = TABLES_BEHIND.index((b, g))
                    sin_b = keep.tile([P, S], BF16, name="sin%d" % tb)
                    nc.sync.dma_start(out=sin_b[:], in_=sin_k[tb, 0, :, :])
                    sin_sb[tb] = sin_b
                    cos_b = keep.tile([P, S], BF16, name="cos%d" % tb)
                    nc.sync.dma_start(out=cos_b[:], in_=cos_k[tb, 0, :, :])
                    cos_sb[tb] = cos_b

        w_codes = keep.tile([P, ROW_TILES, PASSES, P], U32, name="w_codes", align_bytes=64)
        w_scales = keep.tile([P, ROW_TILES, PASSES, P], U8, name="w_scales", align_bytes=64)
        x_codes = keep.tile([P, B, PASSES, S], U32, name="x_codes", align_bytes=64)
        x_scales = keep.tile([P, B, PASSES, S], U8, name="x_scales", align_bytes=64)
        grouped_of = {}
        sums = {}

        def regroup_weights(t):
            words = w_raw[t][:].bitcast(F32).rearrange("m (g p u) -> m g u p", g=PASSES, u=PAIR)
            w_grouped = stage.tile([P, PASSES, P, PACK], BF16, name="w_grouped", align_bytes=64)
            grouped_words = w_grouped[:].rearrange("p g m j -> p (g m j)").bitcast(F32)
            grouped_words = grouped_words.rearrange("p (g m u) -> p g m u", g=PASSES, u=PAIR)
            for first in range(0, PASSES, BANK_PASSES):
                number = 4 + 2 * (t % 2) + first // BANK_PASSES
                bank = psum.tile([P, BANK_PASSES, PAIR, P], F32, name="w_bank", tag="bank%d" % number)
                for i in range(BANK_PASSES):
                    for u in range(PAIR):
                        nc.tensor.transpose(bank[:, i, u, :], words[:, first + i, u, :], identity[:])
                nc.scalar.copy(
                    out=grouped_words[:, first : first + BANK_PASSES, :, :],
                    in_=bank[:].rearrange("p g u m -> p g m u"),
                )
            grouped_of[("w", t)] = w_grouped

        def regroup_chunk(b, g):
            grouped = stage.tile([P, S, PACK], BF16, name="x_grouped", align_bytes=64)
            dst = grouped[:].rearrange("p (c i) j -> p c j i", i=RUN)
            src = x_raw[(b, g)][:].rearrange("p j (c i) -> p c j i", i=RUN)
            cut = SCALAR_POSITIONS[b][g] // RUN
            nc.scalar.copy(out=dst[:, :cut, :, :], in_=src[:, :cut, :, :])
            nc.vector.tensor_copy(out=dst[:, cut:, :, :], in_=src[:, cut:, :, :])
            grouped_of[("x", b, g)] = grouped

        def regroup(unit):
            if unit[0] == "w":
                regroup_weights(unit[1])
            else:
                regroup_chunk(unit[1], unit[2])

        def quantise(unit):
            if unit[0] == "w":
                t = unit[1]
                nc.vector.quantize_mx(
                    out=w_codes[:, t, :, :].rearrange("p g m -> p (g m)").bitcast(FP8X4),
                    scales=w_scales[:, t, :, :].rearrange("p g m -> p (g m)"),
                    in_=grouped_of[unit][:].rearrange("p g m j -> p (g m j)"),
                )
            else:
                b, g = unit[1], unit[2]
                nc.vector.quantize_mx(
                    out=x_codes[:, b, g, :].bitcast(FP8X4),
                    scales=x_scales[:, b, g, :],
                    in_=grouped_of[unit][:].rearrange("p s j -> p (s j)"),
                )

        quantised = set()
        multiplied = set()

        def multiply_what_is_ready(unit):
            quantised.add(unit)
            for b in range(B):
                for g in range(PASSES):
                    for t in range(ROW_TILES):
                        if (b, g, t) in multiplied or ("x", b, g) not in quantised or ("w", t) not in quantised:
                            continue
                        multiplied.add((b, g, t))
                        if g == 0:
                            sums[(b, t)] = psum.tile([P, S], F32, name="sums", tag="bank%d" % (4 * b + t))
                        nc.tensor.matmul_mx(
                            out=sums[(b, t)][:],
                            lhsT=w_codes[:, t, g, :].bitcast(FP8X4),
                            lhsT_scale=w_scales[:, t, g, :],
                            rhs=x_codes[:, b, g, :].bitcast(FP8X4),
                            rhs_scale=x_scales[:, b, g, :],
                            start=(g == 0),
                            stop=(g == PASSES - 1),
                        )

        def store_values(b, half):
            v_sb = values.tile([P, S], F32, name="v_sb")
            nc.scalar.copy(out=v_sb[:], in_=sums[(b, 2 + half)][:])
            nc.sync.dma_start(out=out_1[b, 0, half * P : (half + 1) * P, :], in_=v_sb[:])

        products = {}

        def multiply_by_tables(b, half):
            with_cos = results.tile([P, S], F32, name="with_cos")
            with_sin = results.tile([P, S], F32, name="with_sin")
            nc.vector.tensor_mul(out=with_cos[:], in0=sums[(b, half)][:], in1=cos_sb[b][:])
            nc.vector.tensor_mul(out=with_sin[:], in0=sums[(b, 1 - half)][:], in1=sin_sb[b][:])
            products[(b, half)] = (with_cos, with_sin)

        def combine(engine, b, half):
            with_cos, with_sin = products[(b, half)]
            rotated = results.tile([P, S], F32, name="rotated")
            op = mybir.AluOpType.subtract if half == 0 else mybir.AluOpType.add
            engine.tensor_tensor(out=rotated[:], in0=with_cos[:], in1=with_sin[:], op=op)
            nc.sync.dma_start(out=out_0[b, 0, half * P : (half + 1) * P, :], in_=rotated[:])

        last = len(units) - 1
        for step in range(len(units) + PASS_LAG):
            if step <= last:
                regroup(units[step])
            if step == last:
                store_values(0, 0)
                store_values(0, 1)
            if 1 <= step <= last + 1:
                quantise(units[step - 1])
            if step >= PASS_LAG:
                multiply_what_is_ready(units[step - PASS_LAG])
            if step in (last - 1, last):
                half = step - (last - 1)
                multiply_by_tables(0, half)
                combine(nc.gpsimd, 0, half)

        multiply_by_tables(1, 0)
        store_values(1, 0)
        store_values(1, 1)
        combine(nc.gpsimd, 1, 0)
        multiply_by_tables(1, 1)
        combine(nc.vector, 1, 1)
